import numpy as np
import ml_dtypes


def mxq(x, axis, fmt="e4m3"):
    dtype, down = {"e4m3": (ml_dtypes.float8_e4m3fn, 7), "e5m2": (ml_dtypes.float8_e5m2, 14)}[fmt]
    v = np.moveaxis(np.asarray(x, np.float32).astype(ml_dtypes.bfloat16).astype(np.float64), axis, -1)
    blocks = v.reshape(v.shape[:-1] + (-1, 32))
    amax = np.abs(blocks).max(-1, keepdims=True)
    byte = np.maximum(np.where(amax > 0, np.frexp(amax)[1] - 1 + 127, 0) - down, 1)
    scale = np.exp2(byte - 127.0)
    codes = (blocks / scale).astype(np.float32).astype(dtype).astype(np.float64)
    return np.moveaxis((codes * scale).reshape(v.shape), -1, axis)


WIDE = False


def mx_kscale(k):
    if not WIDE:
        return np.ones(k)
    levels = np.array([10, -10, 5, -5, 0])
    a = np.random.permutation(np.resize(levels, k // 512 * 4)).reshape(k // 512, 4)
    idx = np.arange(k)
    return np.exp2(a[idx // 512, idx % 128 // 32])


BF16 = ml_dtypes.bfloat16


def bf(x):
    return np.asarray(x, np.float32).astype(BF16)


def f64(x):
    return np.asarray(x).astype(np.float64)


E2M1 = np.array([0.0, 0.5, 1.0, 1.5, 2.0, 3.0, 4.0, 6.0, -0.0, -0.5, -1.0, -1.5, -2.0, -3.0, -4.0, -6.0])


def pack_weight(w, fmt):
    k, n = w.shape
    w = f64(bf(w)).reshape(k // 32, 32, n)
    amax = np.abs(w).max(1)
    if fmt == "e4m3":
        byte = np.frexp(amax)[1] - 1 + 127 - 7
    else:
        mant, ex = np.frexp(amax / 6.0)
        byte = np.where(mant > 0.5, ex, ex - 1) + 127
    byte = np.clip(np.where(amax > 0, byte, 1), 1, 254)
    scaled = (w * np.exp2(127.0 - byte)[:, None, :]).reshape(k, n).astype(np.float32)
    by_word = np.ascontiguousarray(scaled.reshape(k // 512, 128, 4, n).transpose(0, 1, 3, 2))
    if fmt == "e4m3":
        words = by_word.astype(ml_dtypes.float8_e4m3fn).view(np.uint8)
    else:
        c = by_word.astype(ml_dtypes.float4_e2m1fn).view(np.uint8) & 0xF
        words = c[..., 0::2] | (c[..., 1::2] << 4)
    return np.ascontiguousarray(words), np.ascontiguousarray(byte.astype(np.uint8).reshape(k // 512, 16, n))


def unpack_weight(words, scales, fmt):
    g, p, n, _ = words.shape
    if fmt == "e4m3":
        vals = np.ascontiguousarray(words).view(ml_dtypes.float8_e4m3fn).astype(np.float64)
    else:
        nib = np.empty((g, p, n, 4), np.uint8)
        nib[..., 0::2] = words & 0xF
        nib[..., 1::2] = words >> 4
        vals = E2M1[nib]
    vals = vals * np.repeat(np.exp2(scales.astype(np.float64) - 127.0), 8, axis=1)[..., None]
    return vals.transpose(0, 1, 3, 2).reshape(g * 512, n)

def pack4(w):
    words, scales = pack_weight(w, "e2m1")
    return words.reshape(words.shape[0], 128, -1), scales


def unpack4(words, scales):
    return unpack_weight(words.reshape(words.shape[0], 128, -1, 2), scales, "e2m1")


B, L, E, H = 4, 1024, 512, 4
HD = E // H
EPS = 1e-12


def l2_normalize(t):
    n = np.sqrt(np.sum(t * t, axis=-1, keepdims=True))
    return t / np.maximum(n, EPS)


def setup_inputs():
    s = mx_kscale(E)
    x = bf(np.random.standard_normal((B, L, E)) * s)
    w = np.random.standard_normal((3 * E, E)) / np.sqrt(E) / s[None, :]
    words, scales = pack4(np.ascontiguousarray(w.T))
    b = bf(np.random.standard_normal(3 * E) * 0.3)
    return {"x": x, "W_words": words, "W_scales": scales, "b": b}


def reference(x, W_words, W_scales, b):
    y = (mxq(f64(x), 2, "e4m3") @ unpack4(W_words, W_scales)) + f64(b)
    y = y.reshape(B, L, H, 3, HD)
    q = np.transpose(y[..., 0, :], (0, 2, 1, 3))
    k = np.transpose(y[..., 1, :], (0, 2, 1, 3))
    v = np.transpose(y[..., 2, :], (0, 2, 1, 3))
    return l2_normalize(q), l2_normalize(k), v

@@ -1,0 +1,178 @@
+from contextlib import ExitStack
+
+import concourse.mybir as mybir
+from concourse.masks import make_identity
+
+BF16 = mybir.dt.bfloat16
+F32 = mybir.dt.float32
+I32 = mybir.dt.int32
+U8 = mybir.dt.uint8
+U32 = mybir.dt.uint32
+FP8X4 = mybir.dt.float8_e4m3fn_x4
+FP4X4 = mybir.dt.float4_e2m1fn_x4
+ACT = mybir.ActivationFunctionType
+ALU = mybir.AluOpType
+
+P = 128
+B, L, E, H = 4, 1024, 512, 4
+HD = E // H
+EPS = 1e-12
+J = L // P
+PAIR = 2
+PAIRS = J // PAIR
+WORDS = E // 2
+BLOCKS = 3 * H
+BANK_BLOCKS = 4
+BANKS = BLOCKS // BANK_BLOCKS
+BANK_COLS = BANK_BLOCKS * HD
+VALUE = 2
+VECTOR_SHARE = 5
+
+FLOPS = 2 * B * L * E * 3 * E
+
+
+def tile_selfattention_pa_t_kernel(tc, x, W_words, W_scales, b, out_0, out_1, out_2):
+    nc = tc.nc
+    outs = [out_0, out_1, out_2]
+
+    with ExitStack() as ctx:
+        ctx.enter_context(tc.manual_schedule())
+        keep = ctx.enter_context(tc.tile_pool(name="keep", bufs=1))
+        grouped_pool = ctx.enter_context(tc.tile_pool(name="grouped", bufs=PAIRS))
+        y_pool = ctx.enter_context(tc.tile_pool(name="y", bufs=6))
+        squares_pool = ctx.enter_context(tc.tile_pool(name="squares", bufs=2))
+        norm_pool = ctx.enter_context(tc.tile_pool(name="norm", bufs=4))
+        xt_psum = ctx.enter_context(tc.psum_pool(name="xt", bufs=PAIRS))
+        acc_psum = ctx.enter_context(tc.psum_pool(name="acc", bufs=4))
+
+        w_scales = keep.tile([P, BLOCKS * HD], U8, align_bytes=64)
+        nc.vector.memset(w_scales[:].bitcast(I32), 0)
+        identity = keep.tile([P, P], F32)
+        make_identity(nc, identity[:])
+        bias = keep.tile([P, BLOCKS, HD], BF16)
+        nc.scalar.dma_start(out=bias[:].rearrange("p i c -> p (i c)"), in_=b.partition_broadcast(P))
+
+        x_sb = keep.tile([P, B, J, E], BF16)
+
+        def load_x(batch, pair):
+            tiles = slice(PAIR * pair, PAIR * (pair + 1))
+            nc.sync.dma_start(
+                out=x_sb[:, batch, tiles, :],
+                in_=x[batch].rearrange("(p j) k -> p j k", j=J)[:, tiles, :],
+            )
+
+        load_x(0, 0)
+        for quadrant in range(4):
+            nc.sync.dma_start(
+                out=w_scales[32 * quadrant : 32 * quadrant + 4, :].bitcast(I32),
+                in_=W_scales[0, 4 * quadrant : 4 * quadrant + 4, :].bitcast(I32),
+            )
+        for pair in range(1, PAIRS):
+            load_x(0, pair)
+        w_words = keep.tile([P, 2 * BLOCKS * HD], U8, align_bytes=64)
+        nc.sync.dma_start(out=w_words[:].bitcast(I32), in_=W_words[0].bitcast(I32))
+        for batch in range(1, B):
+            for pair in range(PAIRS):
+                load_x(batch, pair)
+
+        x_codes = keep.tile([P, B, J * P], U32, align_bytes=64)
+        x_scales = keep.tile([P, B, J * P], U8, align_bytes=64)
+        x_words = x_sb[:].bitcast(F32)
+        grouped_of = {}
+
+        def transpose_batch(batch):
+            for pair in range(PAIRS):
+                xt = xt_psum.tile([P, PAIR, 2, P], F32)
+                for t in range(PAIR):
+                    for u in range(2):
+                        nc.tensor.transpose(
+                            xt[:, t, u, :], x_words[:, batch, PAIR * pair + t, u:WORDS:2], identity[:]
+                        )
+                grouped = grouped_pool.tile([P, PAIR, P, 4], BF16, align_bytes=64)
+                nc.scalar.copy(out=grouped[:].bitcast(F32), in_=xt[:].rearrange("p t u m -> p t m u"))
+                grouped_of[(batch, pair)] = grouped
+
+        def quantise_batch(batch):
+            for pair in range(PAIRS):
+                cols = slice(PAIR * P * pair, PAIR * P * (pair + 1))
+                nc.vector.quantize_mx(
+                    out=x_codes[:, batch, cols].bitcast(FP8X4),
+                    scales=x_scales[:, batch, cols],
+                    in_=grouped_of[(batch, pair)][:].rearrange("p t m k -> p (t m k)"),
+                )
+
+        def store(batch, block, y_block):
+            dest = outs[block % 3][batch, block // 3].rearrange("(p j) c -> p j c", j=J)
+            nc.sync.dma_start(out=dest, in_=y_block)
+
+        def project(batch, bank):
+            blocks = range(BANK_BLOCKS * bank, BANK_BLOCKS * (bank + 1))
+            y_sb = y_pool.tile([P, BANK_BLOCKS, J, HD], F32)
+            squares = squares_pool.tile([P, BANK_BLOCKS, J, HD], BF16)
+            sumsq = norm_pool.tile([P, BANK_BLOCKS, J], F32)
+            normalised = [i for i in range(BANK_BLOCKS) if blocks[i] % 3 != VALUE]
+            for j in range(J):
+                acc = acc_psum.tile([P, BANK_COLS], F32)
+                nc.tensor.matmul_mx(
+                    out=acc[:],
+                    lhsT=x_codes[:, batch, P * j : P * (j + 1)].bitcast(FP8X4),
+                    lhsT_scale=x_scales[:, batch, P * j : P * (j + 1)],
+                    rhs=w_words[:, 2 * BANK_COLS * bank : 2 * BANK_COLS * (bank + 1)].bitcast(FP4X4),
+                    rhs_scale=w_scales[:, BANK_COLS * bank : BANK_COLS * (bank + 1)],
+                    start=True,
+                    stop=True,
+                )
+                nc.vector.tensor_tensor(
+                    out=y_sb[:, :, j, :],
+                    in0=acc[:].rearrange("p (i c) -> p i c", c=HD),
+                    in1=bias[:, blocks[0] : blocks[0] + BANK_BLOCKS, :],
+                    op=ALU.add,
+                )
+                for s, i in enumerate(normalised):
+                    nc.scalar.activation(
+                        out=squares[:, i, j, :],
+                        in_=y_sb[:, i, j, :],
+                        func=ACT.Square,
+                        accum_out=sumsq[:, s, j : j + 1],
+                    )
+            for i in range(BANK_BLOCKS):
+                if i not in normalised:
+                    store(batch, blocks[i], y_sb[:, i, :, :])
+            return {"batch": batch, "blocks": blocks, "normalised": normalised, "y": y_sb, "sumsq": sumsq}
+
+        def reciprocal_norms(unit):
+            count = len(unit["normalised"])
+            inverse = norm_pool.tile([P, BANK_BLOCKS, J], F32)
+            nc.vector.tensor_scalar_max(out=inverse[:, :count, :], in0=unit["sumsq"][:, :count, :], scalar1=EPS * EPS)
+            nc.vector.reciprocal(out=inverse[:, :count, :], in_=inverse[:, :count, :])
+            factor = norm_pool.tile([P, BANK_BLOCKS, J], F32)
+            nc.scalar.activation(out=factor[:, :count, :], in_=inverse[:, :count, :], func=ACT.Sqrt)
+            unit["factor"] = factor
+
+        def scale_and_store(unit):
+            for s, i in enumerate(unit["normalised"]):
+                for j in range(J):
+                    piece = unit["y"][:, i, j, :]
+                    factor = unit["factor"][:, s, j : j + 1]
+                    if j < VECTOR_SHARE:
+                        nc.vector.tensor_scalar_mul(out=piece, in0=piece, scalar1=factor)
+                    else:
+                        nc.scalar.activation(out=piece, in_=piece, func=ACT.Copy, scale=factor)
+                store(unit["batch"], unit["blocks"][i], unit["y"][:, i, :, :])
+
+        transpose_batch(0)
+        quantise_batch(0)
+        order = [(batch, bank) for batch in range(B) for bank in range(BANKS)]
+        units = []
+        for step in range(len(order) + 2):
+            if step < len(order):
+                batch, bank = order[step]
+                units.append(project(batch, bank))
+                if bank == 0 and batch + 1 < B:
+                    transpose_batch(batch + 1)
+                if bank == 1 and batch + 1 < B:
+                    quantise_batch(batch + 1)
+            if 1 <= step <= len(order):
+                reciprocal_norms(units[step - 1])
+            if step >= 2:
+                scale_and_store(units[step - 2])

@@ -21,12 +21,12 @@ J = L // P
 PAIR = 2
 PAIRS = J // PAIR
 WORDS = E // 2
-BLOCKS = 3 * H
-BANK_BLOCKS = 4
-BANKS = BLOCKS // BANK_BLOCKS
-BANK_COLS = BANK_BLOCKS * HD
+PARTS = 3 * H
 VALUE = 2
+BANK_TILES = 4
 VECTOR_SHARE = 5
+NORM_LAG = 2
+SCALE_LAG = 3
 
 FLOPS = 2 * B * L * E * 3 * E
 
@@ -39,17 +39,17 @@ def tile_selfattention_pa_t_kernel(tc, x, W_words, W_scales, b, out_0, out_1, ou
         ctx.enter_context(tc.manual_schedule())
         keep = ctx.enter_context(tc.tile_pool(name="keep", bufs=1))
         grouped_pool = ctx.enter_context(tc.tile_pool(name="grouped", bufs=PAIRS))
-        y_pool = ctx.enter_context(tc.tile_pool(name="y", bufs=6))
-        squares_pool = ctx.enter_context(tc.tile_pool(name="squares", bufs=2))
-        norm_pool = ctx.enter_context(tc.tile_pool(name="norm", bufs=4))
-        xt_psum = ctx.enter_context(tc.psum_pool(name="xt", bufs=PAIRS))
-        acc_psum = ctx.enter_context(tc.psum_pool(name="acc", bufs=4))
+        y_pool = ctx.enter_context(tc.tile_pool(name="y", bufs=12))
+        squares_pool = ctx.enter_context(tc.tile_pool(name="squares", bufs=3))
+        norm_pool = ctx.enter_context(tc.tile_pool(name="norm", bufs=6))
+        xt_psum = ctx.enter_context(tc.psum_pool(name="xt", bufs=2))
+        acc_psum = ctx.enter_context(tc.psum_pool(name="acc", bufs=6))
 
-        w_scales = keep.tile([P, BLOCKS * HD], U8, align_bytes=64)
+        w_scales = keep.tile([P, PARTS * HD], U8, align_bytes=64)
         nc.vector.memset(w_scales[:].bitcast(I32), 0)
         identity = keep.tile([P, P], F32)
         make_identity(nc, identity[:])
-        bias = keep.tile([P, BLOCKS, HD], BF16)
+        bias = keep.tile([P, PARTS, HD], BF16)
         nc.scalar.dma_start(out=bias[:].rearrange("p i c -> p (i c)"), in_=b.partition_broadcast(P))
 
         x_sb = keep.tile([P, B, J, E], BF16)
@@ -69,7 +69,7 @@ def tile_selfattention_pa_t_kernel(tc, x, W_words, W_scales, b, out_0, out_1, ou
             )
         for pair in range(1, PAIRS):
             load_x(0, pair)
-        w_words = keep.tile([P, 2 * BLOCKS * HD], U8, align_bytes=64)
+        w_words = keep.tile([P, 2 * PARTS * HD], U8, align_bytes=64)
         nc.sync.dma_start(out=w_words[:].bitcast(I32), in_=W_words[0].bitcast(I32))
         for batch in range(1, B):
             for pair in range(PAIRS):
@@ -80,99 +80,95 @@ def tile_selfattention_pa_t_kernel(tc, x, W_words, W_scales, b, out_0, out_1, ou
         x_words = x_sb[:].bitcast(F32)
         grouped_of = {}
 
-        def transpose_batch(batch):
-            for pair in range(PAIRS):
-                xt = xt_psum.tile([P, PAIR, 2, P], F32)
-                for t in range(PAIR):
-                    for u in range(2):
-                        nc.tensor.transpose(
-                            xt[:, t, u, :], x_words[:, batch, PAIR * pair + t, u:WORDS:2], identity[:]
-                        )
-                grouped = grouped_pool.tile([P, PAIR, P, 4], BF16, align_bytes=64)
-                nc.scalar.copy(out=grouped[:].bitcast(F32), in_=xt[:].rearrange("p t u m -> p t m u"))
-                grouped_of[(batch, pair)] = grouped
+        def transpose_pair(batch, pair):
+            xt = xt_psum.tile([P, PAIR, 2, P], F32)
+            for t in range(PAIR):
+                for u in range(2):
+                    nc.tensor.transpose(xt[:, t, u, :], x_words[:, batch, PAIR * pair + t, u:WORDS:2], identity[:])
+            grouped = grouped_pool.tile([P, PAIR, P, 4], BF16, align_bytes=64)
+            nc.scalar.copy(out=grouped[:].bitcast(F32), in_=xt[:].rearrange("p t u m -> p t m u"))
+            grouped_of[(batch, pair)] = grouped
 
-        def quantise_batch(batch):
-            for pair in range(PAIRS):
-                cols = slice(PAIR * P * pair, PAIR * P * (pair + 1))
-                nc.vector.quantize_mx(
-                    out=x_codes[:, batch, cols].bitcast(FP8X4),
-                    scales=x_scales[:, batch, cols],
-                    in_=grouped_of[(batch, pair)][:].rearrange("p t m k -> p (t m k)"),
-                )
+        def quantise_pair(batch, pair):
+            cols = slice(PAIR * P * pair, PAIR * P * (pair + 1))
+            nc.vector.quantize_mx(
+                out=x_codes[:, batch, cols].bitcast(FP8X4),
+                scales=x_scales[:, batch, cols],
+                in_=grouped_of[(batch, pair)][:].rearrange("p t m k -> p (t m k)"),
+            )
 
-        def store(batch, block, y_block):
-            dest = outs[block % 3][batch, block // 3].rearrange("(p j) c -> p j c", j=J)
-            nc.sync.dma_start(out=dest, in_=y_block)
+        def store(unit):
+            batch, part = unit["batch"], unit["part"]
+            dest = outs[part % 3][batch, part // 3].rearrange("(p j) c -> p j c", j=J)
+            nc.sync.dma_start(out=dest, in_=unit["y"][:])
 
-        def project(batch, bank):
-            blocks = range(BANK_BLOCKS * bank, BANK_BLOCKS * (bank + 1))
-            y_sb = y_pool.tile([P, BANK_BLOCKS, J, HD], F32)
-            squares = squares_pool.tile([P, BANK_BLOCKS, J, HD], BF16)
-            sumsq = norm_pool.tile([P, BANK_BLOCKS, J], F32)
-            normalised = [i for i in range(BANK_BLOCKS) if blocks[i] % 3 != VALUE]
-            for j in range(J):
-                acc = acc_psum.tile([P, BANK_COLS], F32)
-                nc.tensor.matmul_mx(
-                    out=acc[:],
-                    lhsT=x_codes[:, batch, P * j : P * (j + 1)].bitcast(FP8X4),
-                    lhsT_scale=x_scales[:, batch, P * j : P * (j + 1)],
-                    rhs=w_words[:, 2 * BANK_COLS * bank : 2 * BANK_COLS * (bank + 1)].bitcast(FP4X4),
-                    rhs_scale=w_scales[:, BANK_COLS * bank : BANK_COLS * (bank + 1)],
-                    start=True,
-                    stop=True,
-                )
+        def project(batch, part):
+            y_sb = y_pool.tile([P, J, HD], F32)
+            unit = {"batch": batch, "part": part, "normalised": part % 3 != VALUE, "y": y_sb}
+            for first in range(0, J, BANK_TILES):
+                acc = acc_psum.tile([P, BANK_TILES, HD], F32)
+                for t in range(BANK_TILES):
+                    tokens = slice(P * (first + t), P * (first + t + 1))
+                    nc.tensor.matmul_mx(
+                        out=acc[:, t, :],
+                        lhsT=x_codes[:, batch, tokens].bitcast(FP8X4),
+                        lhsT_scale=x_scales[:, batch, tokens],
+                        rhs=w_words[:, 2 * HD * part : 2 * HD * (part + 1)].bitcast(FP4X4),
+                        rhs_scale=w_scales[:, HD * part : HD * (part + 1)],
+                        start=True,
+                        stop=True,
+                    )
                 nc.vector.tensor_tensor(
-                    out=y_sb[:, :, j, :],
-                    in0=acc[:].rearrange("p (i c) -> p i c", c=HD),
-                    in1=bias[:, blocks[0] : blocks[0] + BANK_BLOCKS, :],
+                    out=y_sb[:, first : first + BANK_TILES, :],
+                    in0=acc[:],
+                    in1=bias[:, part, :].unsqueeze(1).to_broadcast([P, BANK_TILES, HD]),
                     op=ALU.add,
                 )
-                for s, i in enumerate(normalised):
+            if unit["normalised"]:
+                squares = squares_pool.tile([P, J, HD], BF16)
+                sumsq = norm_pool.tile([P, J], F32)
+                for j in range(J):
                     nc.scalar.activation(
-                        out=squares[:, i, j, :],
-                        in_=y_sb[:, i, j, :],
-                        func=ACT.Square,
-                        accum_out=sumsq[:, s, j : j + 1],
+                        out=squares[:, j, :], in_=y_sb[:, j, :], func=ACT.Square, accum_out=sumsq[:, j : j + 1]
                     )
-            for i in range(BANK_BLOCKS):
-                if i not in normalised:
-                    store(batch, blocks[i], y_sb[:, i, :, :])
-            return {"batch": batch, "blocks": blocks, "normalised": normalised, "y": y_sb, "sumsq": sumsq}
+                unit["sumsq"] = sumsq
+            else:
+                store(unit)
+            return unit
 
         def reciprocal_norms(unit):
-            count = len(unit["normalised"])
-            inverse = norm_pool.tile([P, BANK_BLOCKS, J], F32)
-            nc.vector.tensor_scalar_max(out=inverse[:, :count, :], in0=unit["sumsq"][:, :count, :], scalar1=EPS * EPS)
-            nc.vector.reciprocal(out=inverse[:, :count, :], in_=inverse[:, :count, :])
-            factor = norm_pool.tile([P, BANK_BLOCKS, J], F32)
-            nc.scalar.activation(out=factor[:, :count, :], in_=inverse[:, :count, :], func=ACT.Sqrt)
+            inverse = norm_pool.tile([P, J], F32)
+            nc.vector.tensor_scalar_max(out=inverse[:], in0=unit["sumsq"][:], scalar1=EPS * EPS)
+            nc.vector.reciprocal(out=inverse[:], in_=inverse[:])
+            factor = norm_pool.tile([P, J], F32)
+            nc.scalar.activation(out=factor[:], in_=inverse[:], func=ACT.Sqrt)
             unit["factor"] = factor
 
         def scale_and_store(unit):
-            for s, i in enumerate(unit["normalised"]):
-                for j in range(J):
-                    piece = unit["y"][:, i, j, :]
-                    factor = unit["factor"][:, s, j : j + 1]
-                    if j < VECTOR_SHARE:
-                        nc.vector.tensor_scalar_mul(out=piece, in0=piece, scalar1=factor)
-                    else:
-                        nc.scalar.activation(out=piece, in_=piece, func=ACT.Copy, scale=factor)
-                store(unit["batch"], unit["blocks"][i], unit["y"][:, i, :, :])
+            for j in range(J):
+                piece = unit["y"][:, j, :]
+                factor = unit["factor"][:, j : j + 1]
+                if j < VECTOR_SHARE:
+                    nc.vector.tensor_scalar_mul(out=piece, in0=piece, scalar1=factor)
+                else:
+                    nc.scalar.activation(out=piece, in_=piece, func=ACT.Copy, scale=factor)
+            store(unit)
 
-        transpose_batch(0)
-        quantise_batch(0)
-        order = [(batch, bank) for batch in range(B) for bank in range(BANKS)]
+        for pair in range(PAIRS):
+            transpose_pair(0, pair)
+        for pair in range(PAIRS):
+            quantise_pair(0, pair)
+        order = [(batch, part) for batch in range(B) for part in range(PARTS)]
         units = []
-        for step in range(len(order) + 2):
+        for step in range(len(order) + SCALE_LAG):
             if step < len(order):
-                batch, bank = order[step]
-                units.append(project(batch, bank))
-                if bank == 0 and batch + 1 < B:
-                    transpose_batch(batch + 1)
-                if bank == 1 and batch + 1 < B:
-                    quantise_batch(batch + 1)
-            if 1 <= step <= len(order):
-                reciprocal_norms(units[step - 1])
-            if step >= 2:
-                scale_and_store(units[step - 2])
+                batch, part = order[step]
+                units.append(project(batch, part))
+                if batch + 1 < B and part < PAIRS:
+                    transpose_pair(batch + 1, part)
+                if batch + 1 < B and NORM_LAG <= part < NORM_LAG + PAIRS:
+                    quantise_pair(batch + 1, part - NORM_LAG)
+            if NORM_LAG <= step < len(order) + NORM_LAG and units[step - NORM_LAG]["normalised"]:
+                reciprocal_norms(units[step - NORM_LAG])
+            if step >= SCALE_LAG and units[step - SCALE_LAG]["normalised"]:
+                scale_and_store(units[step - SCALE_LAG])

@@ -36,7 +36,6 @@ def tile_selfattention_pa_t_kernel(tc, x, W_words, W_scales, b, out_0, out_1, ou
     outs = [out_0, out_1, out_2]
 
     with ExitStack() as ctx:
-        ctx.enter_context(tc.manual_schedule())
         keep = ctx.enter_context(tc.tile_pool(name="keep", bufs=1))
         grouped_pool = ctx.enter_context(tc.tile_pool(name="grouped", bufs=PAIRS))
         y_pool = ctx.enter_context(tc.tile_pool(name="y", bufs=12))

@@ -24,9 +24,8 @@ WORDS = E // 2
 PARTS = 3 * H
 VALUE = 2
 BANK_TILES = 4
-VECTOR_SHARE = 5
-NORM_LAG = 2
-SCALE_LAG = 3
+VECTOR_TILES = 3
+SCALAR_TILES = 1
 
 FLOPS = 2 * B * L * E * 3 * E
 
@@ -50,6 +49,9 @@ def tile_selfattention_pa_t_kernel(tc, x, W_words, W_scales, b, out_0, out_1, ou
         make_identity(nc, identity[:])
         bias = keep.tile([P, PARTS, HD], BF16)
         nc.scalar.dma_start(out=bias[:].rearrange("p i c -> p (i c)"), in_=b.partition_broadcast(P))
+        one = keep.tile([P, 1], F32)
+        nc.vector.memset(one[:], 1.0)
+        nc.scalar.activation(out=one[:], in_=one[:], func=ACT.Sqrt)
 
         x_sb = keep.tile([P, B, J, E], BF16)
 
@@ -77,33 +79,23 @@ def tile_selfattention_pa_t_kernel(tc, x, W_words, W_scales, b, out_0, out_1, ou
         x_codes = keep.tile([P, B, J * P], U32, align_bytes=64)
         x_scales = keep.tile([P, B, J * P], U8, align_bytes=64)
         x_words = x_sb[:].bitcast(F32)
-        grouped_of = {}
 
-        def transpose_pair(batch, pair):
+        def quantise_pair(batch, pair):
             xt = xt_psum.tile([P, PAIR, 2, P], F32)
             for t in range(PAIR):
                 for u in range(2):
                     nc.tensor.transpose(xt[:, t, u, :], x_words[:, batch, PAIR * pair + t, u:WORDS:2], identity[:])
             grouped = grouped_pool.tile([P, PAIR, P, 4], BF16, align_bytes=64)
             nc.scalar.copy(out=grouped[:].bitcast(F32), in_=xt[:].rearrange("p t u m -> p t m u"))
-            grouped_of[(batch, pair)] = grouped
-
-        def quantise_pair(batch, pair):
             cols = slice(PAIR * P * pair, PAIR * P * (pair + 1))
             nc.vector.quantize_mx(
                 out=x_codes[:, batch, cols].bitcast(FP8X4),
                 scales=x_scales[:, batch, cols],
-                in_=grouped_of[(batch, pair)][:].rearrange("p t m k -> p (t m k)"),
+                in_=grouped[:].rearrange("p t m k -> p (t m k)"),
             )
-
-        def store(unit):
-            batch, part = unit["batch"], unit["part"]
-            dest = outs[part % 3][batch, part // 3].rearrange("(p j) c -> p j c", j=J)
-            nc.sync.dma_start(out=dest, in_=unit["y"][:])
 
         def project(batch, part):
             y_sb = y_pool.tile([P, J, HD], F32)
-            unit = {"batch": batch, "part": part, "normalised": part % 3 != VALUE, "y": y_sb}
             for first in range(0, J, BANK_TILES):
                 acc = acc_psum.tile([P, BANK_TILES, HD], F32)
                 for t in range(BANK_TILES):
@@ -123,51 +115,39 @@ def tile_selfattention_pa_t_kernel(tc, x, W_words, W_scales, b, out_0, out_1, ou
                     in1=bias[:, part, :].unsqueeze(1).to_broadcast([P, BANK_TILES, HD]),
                     op=ALU.add,
                 )
-            if unit["normalised"]:
-                squares = squares_pool.tile([P, J, HD], BF16)
-                sumsq = norm_pool.tile([P, J], F32)
-                for j in range(J):
-                    nc.scalar.activation(
-                        out=squares[:, j, :], in_=y_sb[:, j, :], func=ACT.Square, accum_out=sumsq[:, j : j + 1]
-                    )
-                unit["sumsq"] = sumsq
-            else:
-                store(unit)
-            return unit
+            return y_sb
 
-        def reciprocal_norms(unit):
+        def normalise(y_sb):
+            squares = squares_pool.tile([P, J, HD], BF16)
+            sumsq = norm_pool.tile([P, J], F32)
+            for j in range(J):
+                nc.scalar.activation(
+                    out=squares[:, j, :], in_=y_sb[:, j, :], func=ACT.Square, accum_out=sumsq[:, j : j + 1]
+                )
             inverse = norm_pool.tile([P, J], F32)
-            nc.vector.tensor_scalar_max(out=inverse[:], in0=unit["sumsq"][:], scalar1=EPS * EPS)
+            nc.vector.tensor_scalar_max(out=inverse[:], in0=sumsq[:], scalar1=EPS * EPS)
             nc.vector.reciprocal(out=inverse[:], in_=inverse[:])
             factor = norm_pool.tile([P, J], F32)
             nc.scalar.activation(out=factor[:], in_=inverse[:], func=ACT.Sqrt)
-            unit["factor"] = factor
-
-        def scale_and_store(unit):
             for j in range(J):
-                piece = unit["y"][:, j, :]
-                factor = unit["factor"][:, j : j + 1]
-                if j < VECTOR_SHARE:
-                    nc.vector.tensor_scalar_mul(out=piece, in0=piece, scalar1=factor)
+                piece = y_sb[:, j, :]
+                if j < VECTOR_TILES:
+                    nc.vector.tensor_scalar_mul(out=piece, in0=piece, scalar1=factor[:, j : j + 1])
+                elif j < VECTOR_TILES + SCALAR_TILES:
+                    nc.scalar.activation(out=piece, in_=piece, func=ACT.Copy, scale=factor[:, j : j + 1])
                 else:
-                    nc.scalar.activation(out=piece, in_=piece, func=ACT.Copy, scale=factor)
-            store(unit)
+                    nc.gpsimd.tensor_scalar(
+                        out=piece, in0=piece, scalar1=factor[:, j : j + 1], scalar2=1.0, op0=ALU.mult, op1=ALU.mult
+                    )
 
-        for pair in range(PAIRS):
-            transpose_pair(0, pair)
         for pair in range(PAIRS):
             quantise_pair(0, pair)
-        order = [(batch, part) for batch in range(B) for part in range(PARTS)]
-        units = []
-        for step in range(len(order) + SCALE_LAG):
-            if step < len(order):
-                batch, part = order[step]
-                units.append(project(batch, part))
+        for batch in range(B):
+            for part in range(PARTS):
+                y_sb = project(batch, part)
+                if part % 3 != VALUE:
+                    normalise(y_sb)
+                dest = outs[part % 3][batch, part // 3].rearrange("(p j) c -> p j c", j=J)
+                nc.sync.dma_start(out=dest, in_=y_sb[:])
                 if batch + 1 < B and part < PAIRS:
-                    transpose_pair(batch + 1, part)
-                if batch + 1 < B and NORM_LAG <= part < NORM_LAG + PAIRS:
-                    quantise_pair(batch + 1, part - NORM_LAG)
-            if NORM_LAG <= step < len(order) + NORM_LAG and units[step - NORM_LAG]["normalised"]:
-                reciprocal_norms(units[step - NORM_LAG])
-            if step >= SCALE_LAG and units[step - SCALE_LAG]["normalised"]:
-                scale_and_store(units[step - SCALE_LAG])
+                    quantise_pair(batch + 1, part)

@@ -24,8 +24,7 @@ WORDS = E // 2
 PARTS = 3 * H
 VALUE = 2
 BANK_TILES = 4
-VECTOR_TILES = 3
-SCALAR_TILES = 1
+VECTOR_TILES = 5
 
 FLOPS = 2 * B * L * E * 3 * E
 
@@ -51,7 +50,7 @@ def tile_selfattention_pa_t_kernel(tc, x, W_words, W_scales, b, out_0, out_1, ou
         nc.scalar.dma_start(out=bias[:].rearrange("p i c -> p (i c)"), in_=b.partition_broadcast(P))
         one = keep.tile([P, 1], F32)
         nc.vector.memset(one[:], 1.0)
-        nc.scalar.activation(out=one[:], in_=one[:], func=ACT.Sqrt)
+        nc.scalar.activation(out=one[:], in_=one[:], func=ACT.Abs_reciprocal_sqrt)
 
         x_sb = keep.tile([P, B, J, E], BF16)
 
@@ -124,21 +123,16 @@ def tile_selfattention_pa_t_kernel(tc, x, W_words, W_scales, b, out_0, out_1, ou
                 nc.scalar.activation(
                     out=squares[:, j, :], in_=y_sb[:, j, :], func=ACT.Square, accum_out=sumsq[:, j : j + 1]
                 )
-            inverse = norm_pool.tile([P, J], F32)
-            nc.vector.tensor_scalar_max(out=inverse[:], in0=sumsq[:], scalar1=EPS * EPS)
-            nc.vector.reciprocal(out=inverse[:], in_=inverse[:])
+            floored = norm_pool.tile([P, J], F32)
+            nc.vector.tensor_scalar_max(out=floored[:], in0=sumsq[:], scalar1=EPS * EPS)
             factor = norm_pool.tile([P, J], F32)
-            nc.scalar.activation(out=factor[:], in_=inverse[:], func=ACT.Sqrt)
+            nc.scalar.activation(out=factor[:], in_=floored[:], func=ACT.Abs_reciprocal_sqrt)
             for j in range(J):
                 piece = y_sb[:, j, :]
                 if j < VECTOR_TILES:
                     nc.vector.tensor_scalar_mul(out=piece, in0=piece, scalar1=factor[:, j : j + 1])
-                elif j < VECTOR_TILES + SCALAR_TILES:
-                    nc.scalar.activation(out=piece, in_=piece, func=ACT.Copy, scale=factor[:, j : j + 1])
                 else:
-                    nc.gpsimd.tensor_scalar(
-                        out=piece, in0=piece, scalar1=factor[:, j : j + 1], scalar2=1.0, op0=ALU.mult, op1=ALU.mult
-                    )
+                    nc.scalar.activation(out=piece, in_=piece, func=ACT.Copy, scale=factor[:, j : j + 1])
 
         for pair in range(PAIRS):
             quantise_pair(0, pair)

@@ -24,7 +24,7 @@ WORDS = E // 2
 PARTS = 3 * H
 VALUE = 2
 BANK_TILES = 4
-VECTOR_TILES = 5
+GPSIMD_TILES = 6
 
 FLOPS = 2 * B * L * E * 3 * E
 
@@ -123,16 +123,19 @@ def tile_selfattention_pa_t_kernel(tc, x, W_words, W_scales, b, out_0, out_1, ou
                 nc.scalar.activation(
                     out=squares[:, j, :], in_=y_sb[:, j, :], func=ACT.Square, accum_out=sumsq[:, j : j + 1]
                 )
-            floored = norm_pool.tile([P, J], F32)
-            nc.vector.tensor_scalar_max(out=floored[:], in0=sumsq[:], scalar1=EPS * EPS)
+            above = norm_pool.tile([P, J], F32)
+            nc.scalar.activation(out=above[:], in_=sumsq[:], func=ACT.Relu, bias=-EPS * EPS)
             factor = norm_pool.tile([P, J], F32)
-            nc.scalar.activation(out=factor[:], in_=floored[:], func=ACT.Abs_reciprocal_sqrt)
-            for j in range(J):
+            nc.scalar.activation(out=factor[:], in_=above[:], func=ACT.Abs_reciprocal_sqrt, bias=EPS * EPS)
+            nc.gpsimd.tensor_tensor(
+                out=y_sb[:, 0:GPSIMD_TILES, :],
+                in0=y_sb[:, 0:GPSIMD_TILES, :],
+                in1=factor[:, 0:GPSIMD_TILES].unsqueeze(2).to_broadcast([P, GPSIMD_TILES, HD]),
+                op=ALU.mult,
+            )
+            for j in range(GPSIMD_TILES, J):
                 piece = y_sb[:, j, :]
-                if j < VECTOR_TILES:
-                    nc.vector.tensor_scalar_mul(out=piece, in0=piece, scalar1=factor[:, j : j + 1])
-                else:
-                    nc.scalar.activation(out=piece, in_=piece, func=ACT.Copy, scale=factor[:, j : j + 1])
+                nc.scalar.activation(out=piece, in_=piece, func=ACT.Copy, scale=factor[:, j : j + 1])
 
         for pair in range(PAIRS):
             quantise_pair(0, pair)

@@ -36,6 +36,7 @@ def tile_selfattention_pa_t_kernel(tc, x, W_words, W_scales, b, out_0, out_1, ou
     with ExitStack() as ctx:
         keep = ctx.enter_context(tc.tile_pool(name="keep", bufs=1))
         grouped_pool = ctx.enter_context(tc.tile_pool(name="grouped", bufs=PAIRS))
+        batch_pool = ctx.enter_context(tc.tile_pool(name="batch", bufs=2))
         y_pool = ctx.enter_context(tc.tile_pool(name="y", bufs=12))
         squares_pool = ctx.enter_context(tc.tile_pool(name="squares", bufs=3))
         norm_pool = ctx.enter_context(tc.tile_pool(name="norm", bufs=6))
@@ -79,18 +80,17 @@ def tile_selfattention_pa_t_kernel(tc, x, W_words, W_scales, b, out_0, out_1, ou
         x_scales = keep.tile([P, B, J * P], U8, align_bytes=64)
         x_words = x_sb[:].bitcast(F32)
 
-        def quantise_pair(batch, pair):
+        def turn_pair(batch, pair, grouped):
             xt = xt_psum.tile([P, PAIR, 2, P], F32)
             for t in range(PAIR):
                 for u in range(2):
                     nc.tensor.transpose(xt[:, t, u, :], x_words[:, batch, PAIR * pair + t, u:WORDS:2], identity[:])
-            grouped = grouped_pool.tile([P, PAIR, P, 4], BF16, align_bytes=64)
-            nc.scalar.copy(out=grouped[:].bitcast(F32), in_=xt[:].rearrange("p t u m -> p t m u"))
-            cols = slice(PAIR * P * pair, PAIR * P * (pair + 1))
+            nc.scalar.copy(out=grouped.bitcast(F32), in_=xt[:].rearrange("p t u m -> p t m u"))
+
+        def quantise(batch, first_pair, pairs, grouped):
+            cols = slice(PAIR * P * first_pair, PAIR * P * (first_pair + pairs))
             nc.vector.quantize_mx(
-                out=x_codes[:, batch, cols].bitcast(FP8X4),
-                scales=x_scales[:, batch, cols],
-                in_=grouped[:].rearrange("p t m k -> p (t m k)"),
+                out=x_codes[:, batch, cols].bitcast(FP8X4), scales=x_scales[:, batch, cols], in_=grouped
             )
 
         def project(batch, part):
@@ -138,7 +138,9 @@ def tile_selfattention_pa_t_kernel(tc, x, W_words, W_scales, b, out_0, out_1, ou
                 nc.scalar.activation(out=piece, in_=piece, func=ACT.Copy, scale=factor[:, j : j + 1])
 
         for pair in range(PAIRS):
-            quantise_pair(0, pair)
+            grouped = grouped_pool.tile([P, PAIR, P, 4], BF16, align_bytes=64)
+            turn_pair(0, pair, grouped[:])
+            quantise(0, pair, 1, grouped[:].rearrange("p t m k -> p (t m k)"))
         for batch in range(B):
             for part in range(PARTS):
                 y_sb = project(batch, part)
@@ -147,4 +149,8 @@ def tile_selfattention_pa_t_kernel(tc, x, W_words, W_scales, b, out_0, out_1, ou
                 dest = outs[part % 3][batch, part // 3].rearrange("(p j) c -> p j c", j=J)
                 nc.sync.dma_start(out=dest, in_=y_sb[:])
                 if batch + 1 < B and part < PAIRS:
-                    quantise_pair(batch + 1, part)
+                    if part == 0:
+                        grouped_batch = batch_pool.tile([P, PAIRS, PAIR, P, 4], BF16, align_bytes=64)
+                    turn_pair(batch + 1, part, grouped_batch[:, part, :, :, :])
+                    if part == PAIRS - 1:
+                        quantise(batch + 1, 0, PAIRS, grouped_batch[:].rearrange("p a t m k -> p (a t m k)"))

@@ -25,6 +25,8 @@ PARTS = 3 * H
 VALUE = 2
 BANK_TILES = 4
 GPSIMD_TILES = 6
+DUO = 2
+DUO_TILES = 2
 
 FLOPS = 2 * B * L * E * 3 * E
 
@@ -37,7 +39,7 @@ def tile_selfattention_pa_t_kernel(tc, x, W_words, W_scales, b, out_0, out_1, ou
         keep = ctx.enter_context(tc.tile_pool(name="keep", bufs=1))
         grouped_pool = ctx.enter_context(tc.tile_pool(name="grouped", bufs=PAIRS))
         batch_pool = ctx.enter_context(tc.tile_pool(name="batch", bufs=2))
-        y_pool = ctx.enter_context(tc.tile_pool(name="y", bufs=12))
+        y_pool = ctx.enter_context(tc.tile_pool(name="y", bufs=7))
         squares_pool = ctx.enter_context(tc.tile_pool(name="squares", bufs=3))
         norm_pool = ctx.enter_context(tc.tile_pool(name="norm", bufs=6))
         xt_psum = ctx.enter_context(tc.psum_pool(name="xt", bufs=2))
@@ -93,25 +95,25 @@ def tile_selfattention_pa_t_kernel(tc, x, W_words, W_scales, b, out_0, out_1, ou
                 out=x_codes[:, batch, cols].bitcast(FP8X4), scales=x_scales[:, batch, cols], in_=grouped
             )
 
-        def project(batch, part):
-            y_sb = y_pool.tile([P, J, HD], F32)
-            for first in range(0, J, BANK_TILES):
-                acc = acc_psum.tile([P, BANK_TILES, HD], F32)
-                for t in range(BANK_TILES):
+        def project(batch, first_part):
+            y_sb = y_pool.tile([P, DUO, J, HD], F32)
+            for first in range(0, J, DUO_TILES):
+                acc = acc_psum.tile([P, DUO_TILES, DUO, HD], F32)
+                for t in range(DUO_TILES):
                     tokens = slice(P * (first + t), P * (first + t + 1))
                     nc.tensor.matmul_mx(
-                        out=acc[:, t, :],
+                        out=acc[:, t, :, :].rearrange("p i c -> p (i c)"),
                         lhsT=x_codes[:, batch, tokens].bitcast(FP8X4),
                         lhsT_scale=x_scales[:, batch, tokens],
-                        rhs=w_words[:, 2 * HD * part : 2 * HD * (part + 1)].bitcast(FP4X4),
-                        rhs_scale=w_scales[:, HD * part : HD * (part + 1)],
+                        rhs=w_words[:, 2 * HD * first_part : 2 * HD * (first_part + DUO)].bitcast(FP4X4),
+                        rhs_scale=w_scales[:, HD * first_part : HD * (first_part + DUO)],
                         start=True,
                         stop=True,
                     )
                 nc.vector.tensor_tensor(
-                    out=y_sb[:, first : first + BANK_TILES, :],
+                    out=y_sb[:, :, first : first + DUO_TILES, :].rearrange("p i t c -> p t i c"),
                     in0=acc[:],
-                    in1=bias[:, part, :].unsqueeze(1).to_broadcast([P, BANK_TILES, HD]),
+                    in1=bias[:, first_part : first_part + DUO, :].unsqueeze(1).to_broadcast([P, DUO_TILES, DUO, HD]),
                     op=ALU.add,
                 )
             return y_sb
@@ -142,15 +144,18 @@ def tile_selfattention_pa_t_kernel(tc, x, W_words, W_scales, b, out_0, out_1, ou
             turn_pair(0, pair, grouped[:])
             quantise(0, pair, 1, grouped[:].rearrange("p t m k -> p (t m k)"))
         for batch in range(B):
-            for part in range(PARTS):
-                y_sb = project(batch, part)
-                if part % 3 != VALUE:
-                    normalise(y_sb)
-                dest = outs[part % 3][batch, part // 3].rearrange("(p j) c -> p j c", j=J)
-                nc.sync.dma_start(out=dest, in_=y_sb[:])
-                if batch + 1 < B and part < PAIRS:
-                    if part == 0:
-                        grouped_batch = batch_pool.tile([P, PAIRS, PAIR, P, 4], BF16, align_bytes=64)
-                    turn_pair(batch + 1, part, grouped_batch[:, part, :, :, :])
-                    if part == PAIRS - 1:
-                        quantise(batch + 1, 0, PAIRS, grouped_batch[:].rearrange("p a t m k -> p (a t m k)"))
+            for first_part in range(0, PARTS, DUO):
+                duo_sb = project(batch, first_part)
+                for i in range(DUO):
+                    part = first_part + i
+                    y_sb = duo_sb[:, i, :, :]
+                    if part % 3 != VALUE:
+                        normalise(y_sb)
+                    dest = outs[part % 3][batch, part // 3].rearrange("(p j) c -> p j c", j=J)
+                    nc.sync.dma_start(out=dest, in_=y_sb)
+                    if batch + 1 < B and part < PAIRS:
+                        if part == 0:
+                            grouped_batch = batch_pool.tile([P, PAIRS, PAIR, P, 4], BF16, align_bytes=64)
+                        turn_pair(batch + 1, part, grouped_batch[:, part, :, :, :])
+                        if part == PAIRS - 1:
+                            quantise(batch + 1, 0, PAIRS, grouped_batch[:].rearrange("p a t m k -> p (a t m k)"))

@@ -25,6 +25,7 @@ PARTS = 3 * H
 VALUE = 2
 BANK_TILES = 4
 GPSIMD_TILES = 6
+VECTOR_TILES = 1
 DUO = 2
 DUO_TILES = 2
 
@@ -43,7 +44,8 @@ def tile_selfattention_pa_t_kernel(tc, x, W_words, W_scales, b, out_0, out_1, ou
         squares_pool = ctx.enter_context(tc.tile_pool(name="squares", bufs=3))
         norm_pool = ctx.enter_context(tc.tile_pool(name="norm", bufs=6))
         xt_psum = ctx.enter_context(tc.psum_pool(name="xt", bufs=2))
-        acc_psum = ctx.enter_context(tc.psum_pool(name="acc", bufs=6))
+        acc_psum = ctx.enter_context(tc.psum_pool(name="acc", bufs=5))
+        zero_psum = ctx.enter_context(tc.psum_pool(name="zero", bufs=1))
 
         w_scales = keep.tile([P, PARTS * HD], U8, align_bytes=64)
         nc.vector.memset(w_scales[:].bitcast(I32), 0)
@@ -54,6 +56,11 @@ def tile_selfattention_pa_t_kernel(tc, x, W_words, W_scales, b, out_0, out_1, ou
         one = keep.tile([P, 1], F32)
         nc.vector.memset(one[:], 1.0)
         nc.scalar.activation(out=one[:], in_=one[:], func=ACT.Abs_reciprocal_sqrt)
+
+        zeros_sb = keep.tile([P, P], BF16)
+        nc.vector.memset(zeros_sb[:], 0.0)
+        zeros_psum = zero_psum.tile([P, HD], F32)
+        nc.tensor.matmul(out=zeros_psum[:], lhsT=zeros_sb[:], rhs=zeros_sb[:], start=True, stop=True)
 
         x_sb = keep.tile([P, B, J, E], BF16)
 
@@ -137,7 +144,12 @@ def tile_selfattention_pa_t_kernel(tc, x, W_words, W_scales, b, out_0, out_1, ou
             )
             for j in range(GPSIMD_TILES, J):
                 piece = y_sb[:, j, :]
-                nc.scalar.activation(out=piece, in_=piece, func=ACT.Copy, scale=factor[:, j : j + 1])
+                if j < GPSIMD_TILES + VECTOR_TILES:
+                    nc.vector.scalar_tensor_tensor(
+                        out=piece, in0=piece, scalar=factor[:, j : j + 1], in1=zeros_psum[:], op0=ALU.mult, op1=ALU.add
+                    )
+                else:
+                    nc.scalar.activation(out=piece, in_=piece, func=ACT.Copy, scale=factor[:, j : j + 1])
 
         for pair in range(PAIRS):
             grouped = grouped_pool.tile([P, PAIR, P, 4], BF16, align_bytes=64)

@@ -51,8 +51,11 @@ def tile_selfattention_pa_t_kernel(tc, x, W_words, W_scales, b, out_0, out_1, ou
         nc.vector.memset(w_scales[:].bitcast(I32), 0)
         identity = keep.tile([P, P], F32)
         make_identity(nc, identity[:])
+        bias_row = keep.tile([P, PARTS * HD], BF16)
+        nc.vector.memset(bias_row[:].bitcast(F32), 0.0)
+        ones = keep.tile([P, P], BF16)
+        nc.vector.memset(ones[:], 1.0)
         bias = keep.tile([P, PARTS, HD], BF16)
-        nc.scalar.dma_start(out=bias[:].rearrange("p i c -> p (i c)"), in_=b.partition_broadcast(P))
         one = keep.tile([P, 1], F32)
         nc.vector.memset(one[:], 1.0)
         nc.scalar.activation(out=one[:], in_=one[:], func=ACT.Abs_reciprocal_sqrt)
@@ -77,6 +80,7 @@ def tile_selfattention_pa_t_kernel(tc, x, W_words, W_scales, b, out_0, out_1, ou
                 out=w_scales[32 * quadrant : 32 * quadrant + 4, :].bitcast(I32),
                 in_=W_scales[0, 4 * quadrant : 4 * quadrant + 4, :].bitcast(I32),
             )
+        nc.sync.dma_start(out=bias_row[0:1, :], in_=b.rearrange("(o n) -> o n", o=1))
         for pair in range(1, PAIRS):
             load_x(0, pair)
         w_words = keep.tile([P, 2 * PARTS * HD], U8, align_bytes=64)
@@ -84,6 +88,19 @@ def tile_selfattention_pa_t_kernel(tc, x, W_words, W_scales, b, out_0, out_1, ou
         for batch in range(1, B):
             for pair in range(PAIRS):
                 load_x(batch, pair)
+
+        def spread_bias(first_part):
+            acc = acc_psum.tile([P, DUO_TILES, DUO, HD], F32)
+            nc.tensor.matmul(
+                out=acc[:].rearrange("p t i c -> p (t i c)"),
+                lhsT=ones[:],
+                rhs=bias_row[:, HD * first_part : HD * (first_part + DUO_TILES * DUO)],
+                start=True,
+                stop=True,
+            )
+            nc.scalar.copy(
+                out=bias[:, first_part : first_part + DUO_TILES * DUO, :], in_=acc[:].rearrange("p t i c -> p (t i) c")
+            )
 
         x_codes = keep.tile([P, B, J * P], U32, align_bytes=64)
         x_scales = keep.tile([P, B, J * P], U8, align_bytes=64)
@@ -151,10 +168,13 @@ def tile_selfattention_pa_t_kernel(tc, x, W_words, W_scales, b, out_0, out_1, ou
                 else:
                     nc.scalar.activation(out=piece, in_=piece, func=ACT.Copy, scale=factor[:, j : j + 1])
 
+        spread_bias(0)
         for pair in range(PAIRS):
             grouped = grouped_pool.tile([P, PAIR, P, 4], BF16, align_bytes=64)
             turn_pair(0, pair, grouped[:])
             quantise(0, pair, 1, grouped[:].rearrange("p t m k -> p (t m k)"))
+        for first_part in range(DUO_TILES * DUO, PARTS, DUO_TILES * DUO):
+            spread_bias(first_part)
         for batch in range(B):
             for first_part in range(0, PARTS, DUO):
                 duo_sb = project(batch, first_part)

@@ -24,8 +24,8 @@ WORDS = E // 2
 PARTS = 3 * H
 VALUE = 2
 BANK_TILES = 4
-GPSIMD_TILES = 6
-VECTOR_TILES = 1
+SHARES = (6, 1)
+LAST_SHARES = {9: (4, 2), 10: (2, 3)}
 DUO = 2
 DUO_TILES = 2
 
@@ -75,14 +75,14 @@ def tile_selfattention_pa_t_kernel(tc, x, W_words, W_scales, b, out_0, out_1, ou
             )
 
         load_x(0, 0)
+        nc.sync.dma_start(out=bias_row[0:1, :], in_=b.rearrange("(o n) -> o n", o=1))
+        for pair in range(1, PAIRS):
+            load_x(0, pair)
         for quadrant in range(4):
             nc.sync.dma_start(
                 out=w_scales[32 * quadrant : 32 * quadrant + 4, :].bitcast(I32),
                 in_=W_scales[0, 4 * quadrant : 4 * quadrant + 4, :].bitcast(I32),
             )
-        nc.sync.dma_start(out=bias_row[0:1, :], in_=b.rearrange("(o n) -> o n", o=1))
-        for pair in range(1, PAIRS):
-            load_x(0, pair)
         w_words = keep.tile([P, 2 * PARTS * HD], U8, align_bytes=64)
         nc.sync.dma_start(out=w_words[:].bitcast(I32), in_=W_words[0].bitcast(I32))
         for batch in range(1, B):
@@ -106,12 +106,15 @@ def tile_selfattention_pa_t_kernel(tc, x, W_words, W_scales, b, out_0, out_1, ou
         x_scales = keep.tile([P, B, J * P], U8, align_bytes=64)
         x_words = x_sb[:].bitcast(F32)
 
-        def turn_pair(batch, pair, grouped):
+        def turn_pair(batch, pair, grouped, on_vector):
             xt = xt_psum.tile([P, PAIR, 2, P], F32)
             for t in range(PAIR):
                 for u in range(2):
                     nc.tensor.transpose(xt[:, t, u, :], x_words[:, batch, PAIR * pair + t, u:WORDS:2], identity[:])
-            nc.scalar.copy(out=grouped.bitcast(F32), in_=xt[:].rearrange("p t u m -> p t m u"))
+            if on_vector:
+                nc.vector.tensor_copy(out=grouped.bitcast(F32), in_=xt[:].rearrange("p t u m -> p t m u"))
+            else:
+                nc.scalar.copy(out=grouped.bitcast(F32), in_=xt[:].rearrange("p t u m -> p t m u"))
 
         def quantise(batch, first_pair, pairs, grouped):
             cols = slice(PAIR * P * first_pair, PAIR * P * (first_pair + pairs))
@@ -142,7 +145,7 @@ def tile_selfattention_pa_t_kernel(tc, x, W_words, W_scales, b, out_0, out_1, ou
                 )
             return y_sb
 
-        def normalise(y_sb):
+        def normalise(y_sb, gpsimd_tiles, vector_tiles):
             squares = squares_pool.tile([P, J, HD], BF16)
             sumsq = norm_pool.tile([P, J], F32)
             for j in range(J):
@@ -154,27 +157,29 @@ def tile_selfattention_pa_t_kernel(tc, x, W_words, W_scales, b, out_0, out_1, ou
             factor = norm_pool.tile([P, J], F32)
             nc.scalar.activation(out=factor[:], in_=above[:], func=ACT.Abs_reciprocal_sqrt, bias=EPS * EPS)
             nc.gpsimd.tensor_tensor(
-                out=y_sb[:, 0:GPSIMD_TILES, :],
-                in0=y_sb[:, 0:GPSIMD_TILES, :],
-                in1=factor[:, 0:GPSIMD_TILES].unsqueeze(2).to_broadcast([P, GPSIMD_TILES, HD]),
+                out=y_sb[:, 0:gpsimd_tiles, :],
+                in0=y_sb[:, 0:gpsimd_tiles, :],
+                in1=factor[:, 0:gpsimd_tiles].unsqueeze(2).to_broadcast([P, gpsimd_tiles, HD]),
                 op=ALU.mult,
             )
-            for j in range(GPSIMD_TILES, J):
+            for j in range(gpsimd_tiles, J):
                 piece = y_sb[:, j, :]
-                if j < GPSIMD_TILES + VECTOR_TILES:
+                if j < gpsimd_tiles + vector_tiles:
                     nc.vector.scalar_tensor_tensor(
                         out=piece, in0=piece, scalar=factor[:, j : j + 1], in1=zeros_psum[:], op0=ALU.mult, op1=ALU.add
                     )
                 else:
                     nc.scalar.activation(out=piece, in_=piece, func=ACT.Copy, scale=factor[:, j : j + 1])
 
-        spread_bias(0)
-        for pair in range(PAIRS):
-            grouped = grouped_pool.tile([P, PAIR, P, 4], BF16, align_bytes=64)
-            turn_pair(0, pair, grouped[:])
-            quantise(0, pair, 1, grouped[:].rearrange("p t m k -> p (t m k)"))
-        for first_part in range(DUO_TILES * DUO, PARTS, DUO_TILES * DUO):
-            spread_bias(first_part)
+        with tc.manual_schedule(engines={mybir.EngineType.PE}):
+            for pair in range(PAIRS):
+                grouped = grouped_pool.tile([P, PAIR, P, 4], BF16, align_bytes=64)
+                turn_pair(0, pair, grouped[:], False)
+                quantise(0, pair, 1, grouped[:].rearrange("p t m k -> p (t m k)"))
+                if pair == 1:
+                    spread_bias(0)
+            for first_part in range(DUO_TILES * DUO, PARTS, DUO_TILES * DUO):
+                spread_bias(first_part)
         for batch in range(B):
             for first_part in range(0, PARTS, DUO):
                 duo_sb = project(batch, first_part)
@@ -182,12 +187,13 @@ def tile_selfattention_pa_t_kernel(tc, x, W_words, W_scales, b, out_0, out_1, ou
                     part = first_part + i
                     y_sb = duo_sb[:, i, :, :]
                     if part % 3 != VALUE:
-                        normalise(y_sb)
+                        shares = LAST_SHARES.get(part, SHARES) if batch == B - 1 else SHARES
+                        normalise(y_sb, shares[0], shares[1])
                     dest = outs[part % 3][batch, part // 3].rearrange("(p j) c -> p j c", j=J)
                     nc.sync.dma_start(out=dest, in_=y_sb)
                     if batch + 1 < B and part < PAIRS:
                         if part == 0:
                             grouped_batch = batch_pool.tile([P, PAIRS, PAIR, P, 4], BF16, align_bytes=64)
-                        turn_pair(batch + 1, part, grouped_batch[:, part, :, :, :])
+                        turn_pair(batch + 1, part, grouped_batch[:, part, :, :, :], False)
                         if part == PAIRS - 1:
                             quantise(batch + 1, 0, PAIRS, grouped_batch[:].rearrange("p a t m k -> p (a t m k)"))

@@ -28,6 +28,8 @@ SHARES = (6, 1)
 LAST_SHARES = {9: (4, 2), 10: (2, 3)}
 DUO = 2
 DUO_TILES = 2
+BANK = 512
+WARM = 4
 
 FLOPS = 2 * B * L * E * 3 * E
 
@@ -47,6 +49,11 @@ def tile_selfattention_pa_t_kernel(tc, x, W_words, W_scales, b, out_0, out_1, ou
         acc_psum = ctx.enter_context(tc.psum_pool(name="acc", bufs=5))
         zero_psum = ctx.enter_context(tc.psum_pool(name="zero", bufs=1))
 
+        zeros_sb = keep.tile([P, BANK], BF16)
+        nc.vector.memset(zeros_sb[:].bitcast(F32), 0.0)
+        zeros_psum = zero_psum.tile([P, BANK], F32)
+        for warm in range(WARM):
+            nc.tensor.matmul(out=zeros_psum[:], lhsT=zeros_sb[:, 0:P], rhs=zeros_sb[:], start=True, stop=True)
         w_scales = keep.tile([P, PARTS * HD], U8, align_bytes=64)
         nc.vector.memset(w_scales[:].bitcast(I32), 0)
         identity = keep.tile([P, P], F32)
@@ -60,10 +67,6 @@ def tile_selfattention_pa_t_kernel(tc, x, W_words, W_scales, b, out_0, out_1, ou
         nc.vector.memset(one[:], 1.0)
         nc.scalar.activation(out=one[:], in_=one[:], func=ACT.Abs_reciprocal_sqrt)
 
-        zeros_sb = keep.tile([P, P], BF16)
-        nc.vector.memset(zeros_sb[:], 0.0)
-        zeros_psum = zero_psum.tile([P, HD], F32)
-        nc.tensor.matmul(out=zeros_psum[:], lhsT=zeros_sb[:], rhs=zeros_sb[:], start=True, stop=True)
 
         x_sb = keep.tile([P, B, J, E], BF16)
 
@@ -166,7 +169,7 @@ def tile_selfattention_pa_t_kernel(tc, x, W_words, W_scales, b, out_0, out_1, ou
                 piece = y_sb[:, j, :]
                 if j < gpsimd_tiles + vector_tiles:
                     nc.vector.scalar_tensor_tensor(
-                        out=piece, in0=piece, scalar=factor[:, j : j + 1], in1=zeros_psum[:], op0=ALU.mult, op1=ALU.add
+                        out=piece, in0=piece, scalar=factor[:, j : j + 1], in1=zeros_psum[:, 0:HD], op0=ALU.mult, op1=ALU.add
                     )
                 else:
                     nc.scalar.activation(out=piece, in_=piece, func=ACT.Copy, scale=factor[:, j : j + 1])

from contextlib import ExitStack

import concourse.mybir as mybir
from concourse.masks import make_identity

BF16 = mybir.dt.bfloat16
F32 = mybir.dt.float32
I32 = mybir.dt.int32
U8 = mybir.dt.uint8
U32 = mybir.dt.uint32
FP8X4 = mybir.dt.float8_e4m3fn_x4
FP4X4 = mybir.dt.float4_e2m1fn_x4
ACT = mybir.ActivationFunctionType
ALU = mybir.AluOpType

P = 128
B, L, E, H = 4, 1024, 512, 4
HD = E // H
EPS = 1e-12
J = L // P
PAIR = 2
PAIRS = J // PAIR
WORDS = E // 2
PARTS = 3 * H
VALUE = 2
BANK_TILES = 4
SHARES = (6, 1)
LAST_SHARES = {9: (4, 2), 10: (2, 3)}
DUO = 2
DUO_TILES = 2
BANK = 512
WARM = 4

FLOPS = 2 * B * L * E * 3 * E


def tile_selfattention_pa_t_kernel(tc, x, W_words, W_scales, b, out_0, out_1, out_2):
    nc = tc.nc
    outs = [out_0, out_1, out_2]

    with ExitStack() as ctx:
        keep = ctx.enter_context(tc.tile_pool(name="keep", bufs=1))
        grouped_pool = ctx.enter_context(tc.tile_pool(name="grouped", bufs=PAIRS))
        batch_pool = ctx.enter_context(tc.tile_pool(name="batch", bufs=2))
        y_pool = ctx.enter_context(tc.tile_pool(name="y", bufs=7))
        squares_pool = ctx.enter_context(tc.tile_pool(name="squares", bufs=3))
        norm_pool = ctx.enter_context(tc.tile_pool(name="norm", bufs=6))
        xt_psum = ctx.enter_context(tc.psum_pool(name="xt", bufs=2))
        acc_psum = ctx.enter_context(tc.psum_pool(name="acc", bufs=5))
        zero_psum = ctx.enter_context(tc.psum_pool(name="zero", bufs=1))

        zeros_sb = keep.tile([P, BANK], BF16)
        nc.vector.memset(zeros_sb[:].bitcast(F32), 0.0)
        zeros_psum = zero_psum.tile([P, BANK], F32)
        for warm in range(WARM):
            nc.tensor.matmul(out=zeros_psum[:], lhsT=zeros_sb[:, 0:P], rhs=zeros_sb[:], start=True, stop=True)
        w_scales = keep.tile([P, PARTS * HD], U8, align_bytes=64)
        nc.vector.memset(w_scales[:].bitcast(I32), 0)
        identity = keep.tile([P, P], F32)
        make_identity(nc, identity[:])
        bias_row = keep.tile([P, PARTS * HD], BF16)
        nc.vector.memset(bias_row[:].bitcast(F32), 0.0)
        ones = keep.tile([P, P], BF16)
        nc.vector.memset(ones[:], 1.0)
        bias = keep.tile([P, PARTS, HD], BF16)
        one = keep.tile([P, 1], F32)
        nc.vector.memset(one[:], 1.0)
        nc.scalar.activation(out=one[:], in_=one[:], func=ACT.Abs_reciprocal_sqrt)


        x_sb = keep.tile([P, B, J, E], BF16)

        def load_x(batch, pair):
            tiles = slice(PAIR * pair, PAIR * (pair + 1))
            nc.sync.dma_start(
                out=x_sb[:, batch, tiles, :],
                in_=x[batch].rearrange("(p j) k -> p j k", j=J)[:, tiles, :],
            )

        load_x(0, 0)
        nc.sync.dma_start(out=bias_row[0:1, :], in_=b.rearrange("(o n) -> o n", o=1))
        for pair in range(1, PAIRS):
            load_x(0, pair)
        for quadrant in range(4):
            nc.sync.dma_start(
                out=w_scales[32 * quadrant : 32 * quadrant + 4, :].bitcast(I32),
                in_=W_scales[0, 4 * quadrant : 4 * quadrant + 4, :].bitcast(I32),
            )
        w_words = keep.tile([P, 2 * PARTS * HD], U8, align_bytes=64)
        nc.sync.dma_start(out=w_words[:].bitcast(I32), in_=W_words[0].bitcast(I32))
        for batch in range(1, B):
            for pair in range(PAIRS):
                load_x(batch, pair)

        def spread_bias(first_part):
            acc = acc_psum.tile([P, DUO_TILES, DUO, HD], F32)
            nc.tensor.matmul(
                out=acc[:].rearrange("p t i c -> p (t i c)"),
                lhsT=ones[:],
                rhs=bias_row[:, HD * first_part : HD * (first_part + DUO_TILES * DUO)],
                start=True,
                stop=True,
            )
            nc.scalar.copy(
                out=bias[:, first_part : first_part + DUO_TILES * DUO, :], in_=acc[:].rearrange("p t i c -> p (t i) c")
            )

        x_codes = keep.tile([P, B, J * P], U32, align_bytes=64)
        x_scales = keep.tile([P, B, J * P], U8, align_bytes=64)
        x_words = x_sb[:].bitcast(F32)

        def turn_pair(batch, pair, grouped, on_vector):
            xt = xt_psum.tile([P, PAIR, 2, P], F32)
            for t in range(PAIR):
                for u in range(2):
                    nc.tensor.transpose(xt[:, t, u, :], x_words[:, batch, PAIR * pair + t, u:WORDS:2], identity[:])
            if on_vector:
                nc.vector.tensor_copy(out=grouped.bitcast(F32), in_=xt[:].rearrange("p t u m -> p t m u"))
            else:
                nc.scalar.copy(out=grouped.bitcast(F32), in_=xt[:].rearrange("p t u m -> p t m u"))

        def quantise(batch, first_pair, pairs, grouped):
            cols = slice(PAIR * P * first_pair, PAIR * P * (first_pair + pairs))
            nc.vector.quantize_mx(
                out=x_codes[:, batch, cols].bitcast(FP8X4), scales=x_scales[:, batch, cols], in_=grouped
            )

        def project(batch, first_part):
            y_sb = y_pool.tile([P, DUO, J, HD], F32)
            for first in range(0, J, DUO_TILES):
                acc = acc_psum.tile([P, DUO_TILES, DUO, HD], F32)
                for t in range(DUO_TILES):
                    tokens = slice(P * (first + t), P * (first + t + 1))
                    nc.tensor.matmul_mx(
                        out=acc[:, t, :, :].rearrange("p i c -> p (i c)"),
                        lhsT=x_codes[:, batch, tokens].bitcast(FP8X4),
                        lhsT_scale=x_scales[:, batch, tokens],
                        rhs=w_words[:, 2 * HD * first_part : 2 * HD * (first_part + DUO)].bitcast(FP4X4),
                        rhs_scale=w_scales[:, HD * first_part : HD * (first_part + DUO)],
                        start=True,
                        stop=True,
                    )
                nc.vector.tensor_tensor(
                    out=y_sb[:, :, first : first + DUO_TILES, :].rearrange("p i t c -> p t i c"),
                    in0=acc[:],
                    in1=bias[:, first_part : first_part + DUO, :].unsqueeze(1).to_broadcast([P, DUO_TILES, DUO, HD]),
                    op=ALU.add,
                )
            return y_sb

        def normalise(y_sb, gpsimd_tiles, vector_tiles):
            squares = squares_pool.tile([P, J, HD], BF16)
            sumsq = norm_pool.tile([P, J], F32)
            for j in range(J):
                nc.scalar.activation(
                    out=squares[:, j, :], in_=y_sb[:, j, :], func=ACT.Square, accum_out=sumsq[:, j : j + 1]
                )
            above = norm_pool.tile([P, J], F32)
            nc.scalar.activation(out=above[:], in_=sumsq[:], func=ACT.Relu, bias=-EPS * EPS)
            factor = norm_pool.tile([P, J], F32)
            nc.scalar.activation(out=factor[:], in_=above[:], func=ACT.Abs_reciprocal_sqrt, bias=EPS * EPS)
            nc.gpsimd.tensor_tensor(
                out=y_sb[:, 0:gpsimd_tiles, :],
                in0=y_sb[:, 0:gpsimd_tiles, :],
                in1=factor[:, 0:gpsimd_tiles].unsqueeze(2).to_broadcast([P, gpsimd_tiles, HD]),
                op=ALU.mult,
            )
            for j in range(gpsimd_tiles, J):
                piece = y_sb[:, j, :]
                if j < gpsimd_tiles + vector_tiles:
                    nc.vector.scalar_tensor_tensor(
                        out=piece, in0=piece, scalar=factor[:, j : j + 1], in1=zeros_psum[:, 0:HD], op0=ALU.mult, op1=ALU.add
                    )
                else:
                    nc.scalar.activation(out=piece, in_=piece, func=ACT.Copy, scale=factor[:, j : j + 1])

        with tc.manual_schedule(engines={mybir.EngineType.PE}):
            for pair in range(PAIRS):
                grouped = grouped_pool.tile([P, PAIR, P, 4], BF16, align_bytes=64)
                turn_pair(0, pair, grouped[:], False)
                quantise(0, pair, 1, grouped[:].rearrange("p t m k -> p (t m k)"))
                if pair == 1:
                    spread_bias(0)
            for first_part in range(DUO_TILES * DUO, PARTS, DUO_TILES * DUO):
                spread_bias(first_part)
        for batch in range(B):
            for first_part in range(0, PARTS, DUO):
                duo_sb = project(batch, first_part)
                for i in range(DUO):
                    part = first_part + i
                    y_sb = duo_sb[:, i, :, :]
                    if part % 3 != VALUE:
                        shares = LAST_SHARES.get(part, SHARES) if batch == B - 1 else SHARES
                        normalise(y_sb, shares[0], shares[1])
                    dest = outs[part % 3][batch, part // 3].rearrange("(p j) c -> p j c", j=J)
                    nc.sync.dma_start(out=dest, in_=y_sb)
                    if batch + 1 < B and part < PAIRS:
                        if part == 0:
                            grouped_batch = batch_pool.tile([P, PAIRS, PAIR, P, 4], BF16, align_bytes=64)
                        turn_pair(batch + 1, part, grouped_batch[:, part, :, :, :], False)
                        if part == PAIRS - 1:
                            quantise(batch + 1, 0, PAIRS, grouped_batch[:].rearrange("p a t m k -> p (a t m k)"))
